import numpy as np
import ml_dtypes


def mxq(x, axis, fmt="e4m3"):
    dtype, down = {"e4m3": (ml_dtypes.float8_e4m3fn, 7), "e5m2": (ml_dtypes.float8_e5m2, 14)}[fmt]
    v = np.moveaxis(np.asarray(x, np.float32).astype(ml_dtypes.bfloat16).astype(np.float64), axis, -1)
    blocks = v.reshape(v.shape[:-1] + (-1, 32))
    amax = np.abs(blocks).max(-1, keepdims=True)
    byte = np.maximum(np.where(amax > 0, np.frexp(amax)[1] - 1 + 127, 0) - down, 1)
    scale = np.exp2(byte - 127.0)
    codes = (blocks / scale).astype(np.float32).astype(dtype).astype(np.float64)
    return np.moveaxis((codes * scale).reshape(v.shape), -1, axis)


WIDE = False


def mx_kscale(k):
    if not WIDE:
        return np.ones(k)
    levels = np.array([10, -10, 5, -5, 0])
    if k % 512:
        return np.exp2(np.random.permutation(np.resize(levels, k // 32))).repeat(32)
    a = np.empty((k // 512, 16))
    for p in range(k // 512):
        a[p, :8] = np.random.permutation(np.resize(levels, 8))
        for g in range(8):
            far = levels[np.abs(levels - a[p, g]) >= 10]
            a[p, g + 8] = far[np.random.randint(len(far))]
    return np.exp2(a.ravel()).repeat(32)


BF16 = ml_dtypes.bfloat16


def bf(x):
    return np.asarray(x, np.float32).astype(BF16)


def f64(x):
    return np.asarray(x).astype(np.float64)


B, S, D_MODEL, N_HEADS, QK_ROPE, QK_NOPE, KV_LORA, V_DIM = 2, 256, 2048, 16, 128, 128, 512, 128
RMS_EPS = 1.1920928955078125e-07
ROPE_BASE = 10000.0


def apply_rope(r):
    freqs = 1.0 / (ROPE_BASE ** (np.arange(0, QK_ROPE, 2) / QK_ROPE))
    t = np.arange(S)[:, None] * freqs[None, :]
    cos = np.cos(t)[None, :, None, :]
    sin = np.sin(t)[None, :, None, :]
    r1 = r[..., 0::2]
    r2 = r[..., 1::2]
    return np.stack([r1 * cos - r2 * sin, r2 * cos + r1 * sin], axis=-1).reshape(r.shape)


def draw0():
    s, t = mx_kscale(D_MODEL), mx_kscale(KV_LORA)
    return {"x": bf(np.random.standard_normal((B, S, D_MODEL)) * s),
            "Wkv_a": bf(np.random.standard_normal((D_MODEL, KV_LORA + QK_ROPE)) / np.sqrt(D_MODEL) / s[:, None]),
            "kv_norm_w": bf((1.0 + 0.1 * np.random.standard_normal(KV_LORA)) * t),
            "Wkv_b": bf(np.random.standard_normal((KV_LORA, N_HEADS * (QK_NOPE + V_DIM))) / np.sqrt(KV_LORA) / t[:, None])}


def core(x, Wkv_a, kv_norm_w, Wkv_b):
    kv = mxq(f64(x), 2, "e4m3") @ mxq(f64(Wkv_a), 0, "e4m3")
    c_kv, k_rope = kv[..., :KV_LORA], kv[..., KV_LORA:]
    k_rope = apply_rope(k_rope.reshape(B, S, 1, QK_ROPE))
    c_kv = c_kv * (1.0 / np.sqrt(np.mean(c_kv * c_kv, axis=-1, keepdims=True) + RMS_EPS)) * f64(kv_norm_w)
    kv = (mxq(c_kv, 2, "e4m3") @ mxq(f64(Wkv_b), 0, "e4m3")).reshape(B, S, N_HEADS, QK_NOPE + V_DIM)
    return kv[..., :QK_NOPE], kv[..., QK_NOPE:], k_rope


def e4m3fn_bytes(y):
    return np.clip(np.asarray(y, np.float64), -448.0, 448.0).astype(np.float32).astype(ml_dtypes.float8_e4m3fn).view(np.uint8)


def e4m3fn_values(b):
    return np.asarray(b, np.uint8).view(ml_dtypes.float8_e4m3fn).astype(np.float64)


def setup_inputs():
    d = draw0()
    x0 = np.asarray(d['Wkv_b']).astype(np.float64)
    s = (np.max(np.abs(x0), axis=(1,), keepdims=True) / 448.0).astype(np.float32)
    out = {}
    for k, v in d.items():
        if k == 'Wkv_b':
            out['Wkv_b_bytes'] = e4m3fn_bytes(x0 / s.astype(np.float64))
            out['Wkv_b_scale'] = s
        else:
            out[k] = v
    return out


def reference(x, Wkv_a, kv_norm_w, Wkv_b_bytes, Wkv_b_scale):
    return core(x, Wkv_a, kv_norm_w, e4m3fn_values(Wkv_b_bytes) * Wkv_b_scale.astype(np.float64))

import math
from contextlib import ExitStack

import concourse.mybir as mybir
from concourse.masks import make_identity

F32 = mybir.dt.float32
BF16 = mybir.dt.bfloat16
I32 = mybir.dt.int32
U32 = mybir.dt.uint32
U8 = mybir.dt.uint8
FP8 = mybir.dt.float8_e4m3fn
FP8X4 = mybir.dt.float8_e4m3fn_x4
ALU = mybir.AluOpType
ACT = mybir.ActivationFunctionType

P = 128
B, S, D, H, LORA, ROPE, HD = 2, 256, 2048, 16, 512, 128, 128
KVW = H * 2 * HD
TOK_TILES = B * S // P
PASSES = D // 512
EPS = 1.1920928955078125e-07
UCOLS = 1024
CH = 512
CHUNKS = KVW // CH
UNITS = ((0,), (1,), (2,), (3,))
QUANT_OF = (0, 1, 2, 3, 5, 5, 6, 7)
FLOPS = 2 * B * S * D * (LORA + ROPE) + 2 * B * S * LORA * KVW
LOADS = "wb0a wb0b a0 a1 a2 x0 a3 x1 wb1 x2 wb2 x3"
ORDER = (
    "W:00s W:01 GT1: W:03 GC1: TS: W:02 GT2: GC2:v AT:00 I:0v AT:10 A:01s A:11v Q:0 A:00s "
    "AT:20 I:1v A:10s A:21s XT:01 AQ:0 XT:00 Q:1 A:20s AT:30 A:31v XC:00 AQ:2 XC:01 XT:11 AQ:1 "
    "A:30s XT:10 XQ:0 XC:11 W:12 W:10s M:00 M:01 W:13 M:02 XT:21 AQ:3 XC:10 XT:20 W:11 XC:21 "
    "M:03 XQ:1 XC:20 I:2v ST:0 M:10 M:11 M:12 W:20s M:13 XQ:2 XT:30 N:0 XT:31 ST:1 Q:2 "
    "NT:0 XC:31 M:20 N:1 M:21 NC:0 M:22 XC:30 W:21 M:23 NT:1 ST:2 NQ:0 XQ:3 O:00 O:01 "
    "NC:1 W:23 M:30 E:00 M:31 NQ:1 M:32 N:2 E:01 O:10 O:02 I:3v E:10 NT:2 M:33 E:02 "
    "O:11 O:12 ST:3 NC:2v Q:3 E:11 N:3 O:13 E:12 O:03 NQ:2 W:22 NT:3 E:13 O:20 W:31 "
    "O:21 E:03 O:22 I:4v O:23 E:20 NC:3 E:23 NQ:3 I:5v E:21 O:32 O:30 O:31 E:32 O:33 "
    "E:30 W:33 E:33 Q:5 E:22 E:31 W:30 O:24 O:35 W:32 E:24 O:04 O:05 B:1v E:04 O:14 "
    "O:34 O:25 E:05 I:6v O:15 E:25 E:34 B:0v E:15 Q:6 E:14 I:7v O:16 E:35 O:06 O:26 "
    "E:16 O:36 E:06 RQ: E:36 Q:7 R:2 R:1 E:26 O:07 O:17 E:07v O:37 E:17 O:27 E:37v "
    "R:0 E:27 R:3 RO: "
)


def tile_multiheadlatentattention_pa_kernel(tc, x, Wkv_a, kv_norm_w, Wkv_b_bytes, Wkv_b_scale, out_0, out_1, out_2):
    nc = tc.nc
    with ExitStack() as ctx:
        keep = ctx.enter_context(tc.tile_pool(name="keep", bufs=1))
        flow = ctx.enter_context(tc.tile_pool(name="flow", bufs=3))
        outs = ctx.enter_context(tc.tile_pool(name="outs", bufs=20))
        psum = ctx.enter_context(tc.psum_pool(name="psum", bufs=1))
        ctx.enter_context(tc.manual_schedule())

        wsc = keep.tile([P, 4], F32, name="wsc")
        nc.scalar.dma_start(out=wsc[:], in_=Wkv_b_scale.rearrange("(p t) o -> p (t o)", t=4))
        w4 = keep.tile([P, P], BF16, name="w4", align_bytes=64)
        nc.gpsimd.memset(w4[:], 0.0)
        nc.scalar.dma_start(out=w4[0:4, :], in_=kv_norm_w.rearrange("(j q) -> j q", q=P))
        wb_view = Wkv_b_bytes.rearrange("(p t) n -> p t n", t=4)
        wa_view = Wkv_a.rearrange("(g p t) n -> g p t n", p=P, t=4)
        xr = {}
        wa2 = [keep.tile([P, 2, 4, LORA + ROPE], BF16, name="wa%d" % g, align_bytes=64) for g in range(PASSES // 2)]
        wb_parts = {"wb0a": (0, 1024, 0, 2), "wb0b": (0, 1024, 2, 4), "wb1": (1024, 2048, 0, 4), "wb2": (2048, 4096, 0, 4)}
        wbb = {n: keep.tile([P, t1 - t0, hi - lo], U8, name=n, align_bytes=64) for n, (lo, hi, t0, t1) in wb_parts.items()}
        for n in LOADS.split():
            if n[0] == "x":
                b, q = divmod(int(n[1]), S // P)
                for h in range(2):
                    tile = outs.tile([P, D // 2], BF16, name="os", align_bytes=64)
                    xr[int(n[1]), h] = tile
                    nc.sync.dma_start(out=tile[:], in_=x[b, q * P:(q + 1) * P, h * (D // 2):(h + 1) * (D // 2)])
            elif n[0] == "a":
                nc.sync.dma_start(out=wa2[int(n[1]) // 2][:, int(n[1]) % 2], in_=wa_view[int(n[1])])
            else:
                lo, hi, t0, t1 = wb_parts[n]
                nc.sync.dma_start(out=wbb[n][:], in_=wb_view[:, t0:t1, lo:hi])

        eps = keep.tile([P, 1], F32, name="eps")
        nc.vector.memset(eps[:], EPS)
        dummy = keep.tile([P, 1], F32, name="dummy")
        nc.scalar.activation(out=dummy[:], in_=eps[:], func=ACT.Sin)
        pos = keep.tile([P, 2], F32, name="pos")
        nc.gpsimd.iota(pos[:], pattern=[[P, 2]], base=0, channel_multiplier=1, allow_small_or_imprecise_dtypes=True)
        ident = keep.tile([P, P], F32, name="ident")
        make_identity(nc, ident[:])
        turns = keep.tile([P, 2, 64], F32, name="turns")
        nc.vector.tensor_scalar(out=turns[:, :, 0:1], in0=pos[:].unsqueeze(2), scalar1=1.0 / (2.0 * math.pi), scalar2=None, op0=ALU.mult)
        for w in (1, 2, 4, 8, 16, 32):
            nc.vector.tensor_scalar(out=turns[:, :, w:2 * w], in0=turns[:, :, 0:w], scalar1=10000.0 ** (-w / 64.0), scalar2=None, op0=ALU.mult)
        angle = keep.tile([P, 2, P], F32, name="angle")
        whole = keep.tile([P, 2, P], I32, name="whole")
        wholef = keep.tile([P, 2, P], F32, name="wholef")
        frac = keep.tile([P, 2, P], F32, name="frac")
        fold = keep.tile([P, 2, P], F32, name="fold")
        flat = turns[:].rearrange("p h i -> p (h i)")
        nc.vector.tensor_scalar(out=angle[:, 0], in0=flat, scalar1=0.25, scalar2=None, op0=ALU.add)
        nc.vector.tensor_copy(out=angle[:, 1], in_=flat)
        nc.vector.tensor_copy(out=whole[:], in_=angle[:])
        nc.vector.tensor_copy(out=wholef[:], in_=whole[:])
        nc.vector.tensor_tensor(out=frac[:], in0=angle[:], in1=wholef[:], op=ALU.subtract)
        nc.vector.scalar_tensor_tensor(out=fold[:], in0=frac[:], scalar=0.5, in1=frac[:], op0=ALU.is_gt, op1=ALU.subtract)
        ident_bf = keep.tile([P, P], BF16, name="ident_bf", align_bytes=64)
        nc.vector.tensor_copy(out=ident_bf[:], in_=ident[:])
        cosine = keep.tile([P, P], F32, name="cosine")
        sine = keep.tile([P, P, 2], F32, name="sine")

        free = ["b0", "b1", "b2", "b3", "b4", "b5", "b6"]
        held = {}

        def bank(key, shape, dt):
            n = free.pop(0)
            t = psum.tile(shape, dt, name=n)
            held[key] = (n, t)
            return t

        def done(key):
            n, t = held[key]
            free.append(n)
            return t

        def use(key):
            return held[key][1]

        sc, vc = nc.scalar.copy, nc.vector.tensor_copy
        gain = keep.tile([P, LORA], BF16, name="gain", align_bytes=64)
        wcol = keep.tile([P, P], BF16, name="wcol", align_bytes=64)
        xc = [keep.tile([P, PASSES, P], U32, name="xc%d" % m, align_bytes=64) for m in range(TOK_TILES)]
        xs = [keep.tile([P, PASSES, P], U8, name="xs%d" % m, align_bytes=64) for m in range(TOK_TILES)]
        xg = {}
        wag = {}
        wac = [keep.tile([P, LORA], U32, name="wac%d" % g, align_bytes=64) for g in range(PASSES)]
        was = [keep.tile([P, LORA], U8, name="was%d" % g, align_bytes=64) for g in range(PASSES)]
        war = keep.tile([P, PASSES, ROPE, 4], BF16, name="war", align_bytes=64)
        warc = keep.tile([P, PASSES, ROPE], U32, name="warc", align_bytes=64)
        wars = keep.tile([P, PASSES, ROPE], U8, name="wars", align_bytes=64)
        rope_acc = psum.tile([P, TOK_TILES, ROPE], F32, name="rope_acc")
        rstd = [keep.tile([P, 1], F32, name="rstd%d" % m) for m in range(TOK_TILES)]
        nb = [keep.tile([P, LORA], BF16, name="nb%d" % m, align_bytes=64) for m in range(TOK_TILES)]
        ng = [keep.tile([P, P, 4], BF16, name="ng%d" % m, align_bytes=64) for m in range(TOK_TILES)]
        ncd = [keep.tile([P, P], U32, name="ncd%d" % m, align_bytes=64) for m in range(TOK_TILES)]
        ncs = [keep.tile([P, P], U8, name="ncs%d" % m, align_bytes=64) for m in range(TOK_TILES)]
        wi = {}

        def gain_turn_1(v):
            nc.tensor.transpose(bank("g1", [P, P], BF16)[:], w4[:], ident_bf[:])

        def gain_copy_1(v):
            (vc if v else sc)(out=wcol[:], in_=done("g1")[:])

        def gain_turn_2(v):
            t = bank("g2", [P, LORA], BF16)
            for j in range(4):
                nc.tensor.transpose(t[:, j * P:(j + 1) * P], wcol[:, j:j + 1].to_broadcast([P, P]), ident_bf[:])

        def gain_copy_2(v):
            (vc if v else sc)(out=gain[:], in_=done("g2")[:])

        def x_turn(v, m, h):
            t = bank(("x", m, h), [P, 2, 2, P], F32)
            words = xr[m, h][:].bitcast(F32)
            for g in range(2):
                for u in range(2):
                    nc.tensor.transpose(t[:, g, u, :], words[:, 256 * g + u:256 * (g + 1):2], ident[:])

        def x_copy(v, m, h):
            if m not in xg:
                tile = flow.tile([P, PASSES, P, 4], BF16, name="xg", align_bytes=64)
                xg[m] = tile
            dst = xg[m][:].rearrange("p g r t -> p (g r t)").bitcast(F32).rearrange("p (g r u) -> p g r u", g=PASSES, u=2)
            (vc if v else sc)(out=dst[:, 2 * h:2 * h + 2], in_=done(("x", m, h))[:].rearrange("p g u r -> p g r u"))

        def x_quant(v, m):
            nc.vector.quantize_mx(out=xc[m][:].rearrange("p g r -> p (g r)").bitcast(FP8X4), scales=xs[m][:].rearrange("p g r -> p (g r)"), in_=xg[m][:].rearrange("p g r t -> p (g r t)"))

        def wag_of(g):
            if g not in wag:
                tile = flow.tile([P, LORA, 4], BF16, name="wag", align_bytes=64)
                wag[g] = tile
            return wag[g]

        def a_turn(v, g, h):
            t = bank(("a", g, h), [P, 1024], BF16)
            for q in range(2):
                c0 = 256 * h + P * q
                nc.tensor.matmul(out=t[:, 512 * q:512 * (q + 1)].rearrange("p (c i t) -> p c t i", i=8, t=4), lhsT=ident_bf[:], rhs=wa2[g // 2][:, g % 2, :, c0:c0 + P].rearrange("p t (c i) -> p c t i", i=8), start=True, stop=True)

        def a_lay(v, g, h):
            cols = slice(256 * h, 256 * (h + 1))
            if ("a", g, h) in held:
                (vc if v == "v" else sc)(out=wag_of(g)[:, cols, :].rearrange("p n t -> p (n t)"), in_=done(("a", g, h))[:])
                return
            (vc if v == "v" else sc)(out=wag_of(g)[:, cols, :].rearrange("p (c i) t -> p c t i", i=4), in_=wa2[g // 2][:, g % 2, :, cols].rearrange("p t (c i) -> p c t i", i=4))

        def b_lay(v, b):
            (vc if v == "v" else sc)(out=war[:, 2 * b:2 * b + 2].rearrange("p g (c i) t -> p g c t i", i=4), in_=wa2[b][:, :, :, LORA:].rearrange("p g t (c i) -> p g c t i", i=4))

        def a_quant(v, g):
            nc.vector.quantize_mx(out=wac[g][:].bitcast(FP8X4), scales=was[g][:], in_=wag[g][:].rearrange("p n t -> p (n t)"))

        def r_quant(v):
            nc.vector.quantize_mx(out=warc[:].rearrange("p g n -> p (g n)").bitcast(FP8X4), scales=wars[:].rearrange("p g n -> p (g n)"), in_=war[:].rearrange("p g n t -> p (g n t)"))

        def mm_latent(v, m, g):
            t = bank(("m", m), [P, LORA], F32) if g == 0 else use(("m", m))
            nc.tensor.matmul_mx(out=t[:], lhsT=xc[m][:, g, :].bitcast(FP8X4), lhsT_scale=xs[m][:, g, :], rhs=wac[g][:].bitcast(FP8X4), rhs_scale=was[g][:], start=(g == 0), stop=(g == PASSES - 1))

        def mm_rope(v, m):
            for g in range(PASSES):
                nc.tensor.matmul_mx(out=rope_acc[:, m, :], lhsT=xc[m][:, g, :].bitcast(FP8X4), lhsT_scale=xs[m][:, g, :], rhs=warc[:, g, :].bitcast(FP8X4), rhs_scale=wars[:, g, :], start=(g == 0), stop=(g == PASSES - 1))

        def stats(v, m):
            junk = flow.tile([P, LORA], BF16, name="junk")
            ss = flow.tile([P, 1], F32, name="ss")
            nc.scalar.activation(out=junk[:], in_=use(("m", m))[:], func=ACT.Square, accum_out=ss[:])
            nc.scalar.activation(out=rstd[m][:], in_=ss[:], func=ACT.Abs_reciprocal_sqrt, scale=1.0 / LORA, bias=eps[:])

        def norm(v, m):
            nc.vector.scalar_tensor_tensor(out=nb[m][:], in0=done(("m", m))[:], scalar=rstd[m][:], in1=gain[:], op0=ALU.mult, op1=ALU.mult)

        def n_turn(v, m):
            t = bank(("n", m), [P, 2, P], F32)
            words = nb[m][:].bitcast(F32)
            for u in range(2):
                nc.tensor.transpose(t[:, u, :], words[:, u::2], ident[:])

        def n_copy(v, m):
            (vc if v else sc)(out=ng[m][:].rearrange("p r t -> p (r t)").bitcast(F32).rearrange("p (r u) -> p r u", u=2), in_=done(("n", m))[:].rearrange("p u r -> p r u"))

        def n_quant(v, m):
            nc.vector.quantize_mx(out=ncd[m][:].bitcast(FP8X4), scales=ncs[m][:], in_=ng[m][:].rearrange("p r t -> p (r t)"))

        wf = [keep.tile([P, 4, UCOLS * len(us)], BF16, name="wf%d" % w, align_bytes=64) for w, us in enumerate(UNITS)]

        def widen(v, w, t):
            lo = UNITS[w][0] * UCOLS
            cols = UCOLS * len(UNITS[w])
            for n, (a, b, t0, t1) in wb_parts.items():
                if a <= lo < b and t0 <= t < t1:
                    view = wbb[n][:, t - t0, lo - a:lo - a + cols].bitcast(FP8)
            if v == "s":
                nc.scalar.activation(out=wf[w][:, t, :], in_=view, func=ACT.Copy, scale=wsc[:, t:t + 1])
            else:
                nc.vector.tensor_scalar(out=wf[w][:, t, :], in0=view, scalar1=wsc[:, t:t + 1], scalar2=None, op0=ALU.mult)

        def planes_of(c):
            u, s = divmod(c, 2)
            w = [k for k, us in enumerate(UNITS) if u in us][0]
            lo = UCOLS * UNITS[w].index(u)
            return wf[w][:, :, lo:lo + UCOLS].rearrange("p t (h s d) -> p s t h d", s=2, d=HD)[:, s]

        def wi_of(c):
            members = [k for k in range(CHUNKS) if QUANT_OF[k] == QUANT_OF[c]]
            if members[-1] not in wi:
                tile = flow.tile([P, CH * len(members), 4], BF16, name="wi%d" % len(members), align_bytes=64, bufs=2)
                wi[members[-1]] = tile
            lo = CH * members.index(c)
            return wi[members[-1]][:, lo:lo + CH, :]

        def i_turn(v, c, k):
            t = bank(("i", c, k), [P, 1024], BF16)
            for q in range(2):
                nc.tensor.matmul(out=t[:, 512 * q:512 * (q + 1)].rearrange("p (c i t) -> p c t i", i=8, t=4), lhsT=ident_bf[:], rhs=planes_of(c)[:, :, 2 * k + q].rearrange("p t (c i) -> p c t i", i=8), start=True, stop=True)

        def i_copy(v, c, k):
            (vc if v == "v" else sc)(out=wi_of(c)[:, 256 * k:256 * (k + 1), :].rearrange("p n t -> p (n t)"), in_=done(("i", c, k))[:])

        def i_copy_0(v, c):
            i_copy(v, c, 0)

        def interleave(v, c):
            if ("i", c, 1) in held:
                i_copy(v, c, 1)
                return
            vc(out=wi_of(c).rearrange("p (h c i) t -> p h c t i", h=4, i=4), in_=planes_of(c).rearrange("p t h (c i) -> p h c t i", i=4))

        wbc = {}
        wbs = {}

        def wb_quant(v, c):
            cols = wi[c].shape[1]
            codes = keep.tile([P, cols], U32, name="wbc%d" % c, align_bytes=64)
            planes = keep.tile([P, cols], U8, name="wbs%d" % c, align_bytes=64)
            wbc[c] = codes
            wbs[c] = planes
            nc.vector.quantize_mx(out=codes[:].bitcast(FP8X4), scales=planes[:], in_=wi[c][:].rearrange("p n t -> p (n t)"))

        def mm_out(v, m, c):
            members = [k for k in range(CHUNKS) if QUANT_OF[k] == QUANT_OF[c]]
            cols = slice(CH * members.index(c), CH * members.index(c) + CH)
            nc.tensor.matmul_mx(out=bank(("o", m, c), [P, CH], F32)[:], lhsT=ncd[m][:].bitcast(FP8X4), lhsT_scale=ncs[m][:], rhs=wbc[QUANT_OF[c]][:, cols].bitcast(FP8X4), rhs_scale=wbs[QUANT_OF[c]][:, cols], start=True, stop=True)

        def out_copy(v, m, c):
            u, s = divmod(c, 2)
            b, q = divmod(m, S // P)
            dst = (out_0, out_1)[s][b, q * P:(q + 1) * P].rearrange("p h d -> p (h d)")
            tile = outs.tile([P, CH], F32, name="os", align_bytes=64)
            (vc if v else sc)(out=tile[:], in_=done(("o", m, c))[:])
            nc.sync.dma_start(out=dst[:, CH * u:CH * (u + 1)], in_=tile[:])

        def trig_s(v):
            nc.scalar.activation(out=cosine[:], in_=fold[:, 0], func=ACT.Sin, scale=-2.0 * math.pi)
            nc.scalar.activation(out=sine[:, :, 0], in_=fold[:, 1], func=ACT.Sin, scale=2.0 * math.pi)
            nc.scalar.activation(out=sine[:, :, 1], in_=fold[:, 1], func=ACT.Sin, scale=-2.0 * math.pi)
            nc.scalar.activation(out=dummy[:], in_=eps[:], func=ACT.Abs_reciprocal_sqrt, scale=1.0 / LORA, bias=eps[:])

        def rope_out(v):
            pc = keep.tile([P, TOK_TILES, ROPE], F32, name="pc")
            psn = keep.tile([P, TOK_TILES, ROPE], F32, name="psn")
            kr = keep.tile([P, TOK_TILES, ROPE], F32, name="kr")
            view = rope_acc[:].rearrange("p (b h) (i e) -> p b (h i) e", b=B, e=2)
            nc.vector.tensor_tensor(out=pc[:].rearrange("p (b h) (i e) -> p b (h i) e", b=B, e=2), in0=view, in1=cosine[:].unsqueeze(1).unsqueeze(3).to_broadcast([P, B, P, 2]), op=ALU.mult)
            nc.vector.tensor_tensor(out=psn[:].rearrange("p (b h) (i e) -> p b (h i) e", b=B, e=2), in0=view[:, :, :, ::-1], in1=sine[:].unsqueeze(1).to_broadcast([P, B, P, 2]), op=ALU.mult)
            nc.vector.tensor_tensor(out=kr[:], in0=pc[:], in1=psn[:], op=ALU.add)
            nc.sync.dma_start(out=out_2.rearrange("b (q p) o d -> p (b q) (o d)", p=P), in_=kr[:])

        steps = {
            "GT1": gain_turn_1, "GC1": gain_copy_1, "GT2": gain_turn_2, "GC2": gain_copy_2,
            "XT": x_turn, "XC": x_copy, "XQ": x_quant, "AT": a_turn, "A": a_lay, "B": b_lay, "AQ": a_quant,
            "RQ": r_quant, "M": mm_latent, "R": mm_rope, "ST": stats, "N": norm, "NT": n_turn, "NC": n_copy,
            "NQ": n_quant, "W": widen, "IT": i_turn, "J": i_copy_0, "I": interleave, "Q": wb_quant, "O": mm_out, "E": out_copy,
            "TS": trig_s, "RO": rope_out,
        }
        for word in ORDER.split():
            name, args = word.split(":")
            flag = args[-1:] if args[-1:] in ("v", "s") else ""
            steps[name](flag, *[int(a) for a in args if a not in "vs"])
